import numpy as np
import ml_dtypes

BF16 = ml_dtypes.bfloat16


def bf(x):
    return np.asarray(x, np.float32).astype(BF16)


def f32(x):
    return np.asarray(x, np.float32)


def f64(x):
    return np.asarray(x).astype(np.float64)


def striped(idx):
    return np.tile(idx.reshape(-1, 16).T, (8, 1))


D, S, H, FI, FO, R, N = 128, 512, 128, 128, 128, 2, 1024
ALPHA = 1.0


def silu(v):
    return v / (1.0 + np.exp(-v))


def setup_inputs():
    return {
        "styles": bf(np.random.standard_normal((D, S))),
        "w1": bf(np.random.standard_normal((D, H)) / np.sqrt(D)),
        "b1": f32(0.1 * np.random.standard_normal((H, 1))),
        "w2": bf(0.5 * np.random.standard_normal((H, (FI + FO) * R)) / np.sqrt(H)),
        "b2": f32(0.1 * np.random.standard_normal(((FI + FO) * R, 1))),
        "x": bf(np.random.standard_normal((FI, N))),
        "wb": bf(np.random.standard_normal((FI, FO)) / np.sqrt(FI)),
        "bb": f32(0.1 * np.random.standard_normal((FO, 1))),
        "offs": striped(np.random.permutation(np.tile(np.arange(S), 2))[:N]),
    }


def reference(styles, w1, b1, w2, b2, x, wb, bb, offs):
    idx = offs[:16].T.reshape(-1)
    h = silu(f64(w1).T @ f64(styles)[:, idx] + f64(b1))
    p = f64(w2).T @ h + f64(b2)
    a = p[:FI * R].reshape(R, FI, N)
    bm = p[FI * R:].reshape(R, FO, N)
    low = (a * f64(x)[None]).sum(axis=1)
    delta = (low[:, None, :] * bm).sum(axis=0)
    return f64(wb).T @ f64(x) + f64(bb) + ALPHA * delta

@@ -1,0 +1,133 @@
+import concourse.mybir as mybir
+from concourse.masks import make_identity
+
+P = 128
+S = 512
+N = 1024
+R = 2
+PIECE = 256
+N_PIECES = N // PIECE
+WARM_UP = 3
+WARM_COLS = 512
+BF16, F32, U16 = mybir.dt.bfloat16, mybir.dt.float32, mybir.dt.uint16
+ADD, MULT = mybir.AluOpType.add, mybir.AluOpType.mult
+SILU, IDENTITY = mybir.ActivationFunctionType.Silu, mybir.ActivationFunctionType.Identity
+
+FLOPS = 2 * N * (P * P + P * 2 * R * P + P * P) + 4 * R * P * N
+
+
+def tile_stylehyperlinear_kernel(tc, styles, w1, b1, w2, b2, x, wb, bb, offs, out):
+    nc = tc.nc
+    with (
+        tc.tile_pool(name="held", bufs=1) as held,
+        tc.tile_pool(name="work", bufs=N_PIECES) as work,
+        tc.psum_pool(name="psum", bufs=8) as psum,
+    ):
+        offsets = held.tile([P, N // 16], U16, name="offsets")
+        nc.sync.dma_start(offsets[:], offs)
+        bank = held.tile([P, S], BF16, name="bank")
+        nc.scalar.dma_start(bank[:], styles)
+        w1_sb = held.tile([P, P], BF16, name="w1_sb")
+        nc.sync.dma_start(w1_sb[:], w1)
+        b1_sb = held.tile([P, 1], F32, name="b1_sb")
+        nc.scalar.dma_start(b1_sb[:], b1)
+        w2_sb = held.tile([P, 2 * R * P], BF16, name="w2_sb")
+        nc.sync.dma_start(w2_sb[:], w2)
+        b2_sb = held.tile([P, 2 * R], F32, name="b2_sb")
+        with nc.allow_non_contiguous_dma(reason="512 biases, one to a partition and block"):
+            nc.scalar.dma_start(b2_sb[:], b2.rearrange("(q p) one -> p (q one)", p=P))
+        x_half = [held.tile([P, N // 2], BF16, name=f"x_half{i}") for i in range(2)]
+        nc.sync.dma_start(x_half[0][:], x[:, 0 : N // 2])
+        bb_sb = held.tile([P, 1], F32, name="bb_sb")
+        nc.scalar.dma_start(bb_sb[:], bb)
+        nc.gpsimd.dma_start(x_half[1][:], x[:, N // 2 : N])
+        wb_sb = held.tile([P, P], BF16, name="wb_sb")
+        nc.gpsimd.dma_start(wb_sb[:], wb)
+
+        ones = held.tile([P, WARM_COLS], BF16, name="ones")
+        nc.vector.memset(ones[:], 1.0)
+        scratch = held.tile([P, 1], BF16, name="scratch")
+        nc.scalar.activation(scratch[:], ones[:, 0:1], SILU)
+        identity = held.tile([P, P], F32, name="identity")
+        make_identity(nc, identity[:])
+        idle = psum.tile([P, WARM_COLS], F32, name="idle", tag="bank")
+        for i in range(WARM_UP):
+            nc.tensor.matmul(idle[:], ones[:, 0:P], ones[:], start=True, stop=True)
+
+        def bank_tile(name, columns):
+            return psum.tile([P, columns], F32, name=name, tag="bank")
+
+        z = [bank_tile(f"z{c}", PIECE) for c in range(N_PIECES)]
+        for c in range(N_PIECES):
+            looked_up = bank[:].indirect(offsets[:, c * (PIECE // 16) : (c + 1) * (PIECE // 16)])
+            nc.tensor.matmul(z[c][:], w1_sb[:], looked_up, start=True, stop=True)
+
+        h = [work.tile([P, PIECE], BF16, name="h") for c in range(N_PIECES)]
+        for c in range(N_PIECES):
+            nc.scalar.activation(h[c][:], z[c][:], SILU, bias=b1_sb[:])
+
+        def ranks():
+            return [(r, slice(r * PIECE, (r + 1) * PIECE)) for r in range(R)]
+
+        def x_piece(c):
+            return x_half[c * PIECE // (N // 2)][:, c * PIECE % (N // 2) : c * PIECE % (N // 2) + PIECE]
+
+        prod, vec, low, base, base_sb = {}, {}, {}, {}, {}
+
+        summer = ["vector" if c >= N_PIECES // 2 else "gpsimd" if c % 2 == 0 else "tensor" for c in range(N_PIECES)]
+
+        def input_vectors(c):
+            prod[c] = work.tile([P, R * PIECE], BF16, name="prod")
+            for r, rank in ranks():
+                p_in = bank_tile(f"p_in{r}", PIECE)
+                nc.tensor.matmul(p_in[:], w2_sb[:, r * P : (r + 1) * P], h[c][:], start=True, stop=True)
+                if r == R - 1 and 0 < c < N_PIECES - 1:
+                    moved = work.tile([P, PIECE], F32, name="moved")
+                    nc.scalar.activation(moved[:], p_in[:], IDENTITY, bias=b2_sb[:, r : r + 1])
+                    nc.gpsimd.tensor_tensor(prod[c][:, rank], moved[:], x_piece(c), MULT)
+                else:
+                    nc.vector.scalar_tensor_tensor(
+                        prod[c][:, rank], p_in[:], b2_sb[:, r : r + 1], x_piece(c), op0=ADD, op1=MULT
+                    )
+
+        def output_vectors(c):
+            p_out = bank_tile("p_out", R * PIECE)
+            vec[c] = work.tile([P, R * PIECE], F32, name="vec")
+            for r, rank in ranks():
+                nc.tensor.matmul(p_out[:, rank], w2_sb[:, (R + r) * P : (R + r + 1) * P], h[c][:], start=True, stop=True)
+            for r, rank in ranks():
+                nc.scalar.activation(vec[c][:, rank], p_out[:, rank], IDENTITY, bias=b2_sb[:, R + r : R + r + 1])
+
+        def sums_over_features(c):
+            low[c] = bank_tile("low", R * PIECE)
+            nc.tensor.matmul(low[c][:], ones[:, 0:P], prod[c][:], start=True, stop=True)
+            base[c] = bank_tile("base", PIECE)
+            nc.tensor.matmul(base[c][:], wb_sb[:], x_piece(c), start=True, stop=summer[c] != "tensor")
+            if summer[c] == "gpsimd":
+                base_sb[c] = work.tile([P, PIECE], F32, name="base_sb")
+                nc.scalar.activation(base_sb[c][:], base[c][:], IDENTITY, bias=bb_sb[:])
+
+        def finish(c):
+            term = work.tile([P, R * PIECE], F32, name="term")
+            nc.vector.tensor_tensor(term[:], low[c][:], vec[c][:], MULT)
+            res = work.tile([P, PIECE], F32, name="res")
+            if summer[c] == "tensor":
+                for r, rank in ranks():
+                    nc.tensor.matmul(base[c][:], identity[:], term[:, rank], start=False, stop=r == R - 1)
+                nc.scalar.activation(res[:], base[c][:], IDENTITY, bias=bb_sb[:])
+            elif summer[c] == "gpsimd":
+                delta = work.tile([P, PIECE], F32, name="delta")
+                nc.gpsimd.tensor_tensor(delta[:], term[:, 0:PIECE], term[:, PIECE : 2 * PIECE], ADD)
+                nc.gpsimd.tensor_tensor(res[:], delta[:], base_sb[c][:], ADD)
+            else:
+                part = work.tile([P, PIECE], F32, name="part")
+                nc.vector.scalar_tensor_tensor(part[:], base[c][:], bb_sb[:], term[:, 0:PIECE], op0=ADD, op1=ADD)
+                adder = nc.gpsimd if c + 1 < N_PIECES else nc.vector
+                adder.tensor_tensor(res[:], part[:], term[:, PIECE : 2 * PIECE], ADD)
+            nc.sync.dma_start(out[:, c * PIECE : (c + 1) * PIECE], res[:])
+
+        stages = [input_vectors, output_vectors, sums_over_features, finish]
+        for step in range(N_PIECES + len(stages) - 1):
+            for behind, stage in enumerate(stages):
+                if 0 <= step - behind < N_PIECES:
+                    stage(step - behind)

@@ -7,8 +7,7 @@ N = 1024
 R = 2
 PIECE = 256
 N_PIECES = N // PIECE
-WARM_UP = 3
-WARM_COLS = 512
+WARM_UP = 12
 BF16, F32, U16 = mybir.dt.bfloat16, mybir.dt.float32, mybir.dt.uint16
 ADD, MULT = mybir.AluOpType.add, mybir.AluOpType.mult
 SILU, IDENTITY = mybir.ActivationFunctionType.Silu, mybir.ActivationFunctionType.Identity
@@ -26,33 +25,37 @@ def tile_stylehyperlinear_kernel(tc, styles, w1, b1, w2, b2, x, wb, bb, offs, ou
         offsets = held.tile([P, N // 16], U16, name="offsets")
         nc.sync.dma_start(offsets[:], offs)
         bank = held.tile([P, S], BF16, name="bank")
-        nc.scalar.dma_start(bank[:], styles)
+        nc.sync.dma_start(bank[:], styles)
         w1_sb = held.tile([P, P], BF16, name="w1_sb")
         nc.sync.dma_start(w1_sb[:], w1)
         b1_sb = held.tile([P, 1], F32, name="b1_sb")
-        nc.scalar.dma_start(b1_sb[:], b1)
-        w2_sb = held.tile([P, 2 * R * P], BF16, name="w2_sb")
-        nc.sync.dma_start(w2_sb[:], w2)
+        nc.sync.dma_start(b1_sb[:], b1)
+        w2_in = held.tile([P, R * P], BF16, name="w2_in")
+        nc.sync.dma_start(w2_in[:], w2[:, 0 : R * P])
         b2_sb = held.tile([P, 2 * R], F32, name="b2_sb")
         with nc.allow_non_contiguous_dma(reason="512 biases, one to a partition and block"):
-            nc.scalar.dma_start(b2_sb[:], b2.rearrange("(q p) one -> p (q one)", p=P))
-        x_half = [held.tile([P, N // 2], BF16, name=f"x_half{i}") for i in range(2)]
-        nc.sync.dma_start(x_half[0][:], x[:, 0 : N // 2])
-        bb_sb = held.tile([P, 1], F32, name="bb_sb")
-        nc.scalar.dma_start(bb_sb[:], bb)
-        nc.gpsimd.dma_start(x_half[1][:], x[:, N // 2 : N])
+            nc.sync.dma_start(b2_sb[:], b2.rearrange("(q p) one -> p (q one)", p=P))
+        x_cuts = [0, PIECE, 2 * PIECE, N]
+        x_sb = [held.tile([P, x_cuts[i + 1] - x_cuts[i]], BF16, name=f"x_sb{i}") for i in range(3)]
+        nc.sync.dma_start(x_sb[0][:], x[:, 0 : x_cuts[1]])
+        nc.gpsimd.dma_start(x_sb[1][:], x[:, x_cuts[1] : x_cuts[2]])
+        w2_out = held.tile([P, R * P], BF16, name="w2_out")
+        nc.sync.dma_start(w2_out[:], w2[:, R * P : 2 * R * P])
+        nc.gpsimd.dma_start(x_sb[2][:], x[:, x_cuts[2] : N])
         wb_sb = held.tile([P, P], BF16, name="wb_sb")
-        nc.gpsimd.dma_start(wb_sb[:], wb)
+        nc.sync.dma_start(wb_sb[:], wb)
+        bb_sb = held.tile([P, 1], F32, name="bb_sb")
+        nc.sync.dma_start(bb_sb[:], bb)
 
-        ones = held.tile([P, WARM_COLS], BF16, name="ones")
+        ones = held.tile([P, P], BF16, name="ones")
         nc.vector.memset(ones[:], 1.0)
         scratch = held.tile([P, 1], BF16, name="scratch")
         nc.scalar.activation(scratch[:], ones[:, 0:1], SILU)
         identity = held.tile([P, P], F32, name="identity")
         make_identity(nc, identity[:])
-        idle = psum.tile([P, WARM_COLS], F32, name="idle", tag="bank")
+        idle = psum.tile([P, P], F32, name="idle", tag="bank")
         for i in range(WARM_UP):
-            nc.tensor.matmul(idle[:], ones[:, 0:P], ones[:], start=True, stop=True)
+            nc.tensor.matmul(idle[:], ones[:], ones[:], start=True, stop=True)
 
         def bank_tile(name, columns):
             return psum.tile([P, columns], F32, name=name, tag="bank")
@@ -70,7 +73,9 @@ def tile_stylehyperlinear_kernel(tc, styles, w1, b1, w2, b2, x, wb, bb, offs, ou
             return [(r, slice(r * PIECE, (r + 1) * PIECE)) for r in range(R)]
 
         def x_piece(c):
-            return x_half[c * PIECE // (N // 2)][:, c * PIECE % (N // 2) : c * PIECE % (N // 2) + PIECE]
+            load = min(c, 2)
+            first = c * PIECE - x_cuts[load]
+            return x_sb[load][:, first : first + PIECE]
 
         prod, vec, low, base, base_sb = {}, {}, {}, {}, {}
 
@@ -80,7 +85,7 @@ def tile_stylehyperlinear_kernel(tc, styles, w1, b1, w2, b2, x, wb, bb, offs, ou
             prod[c] = work.tile([P, R * PIECE], BF16, name="prod")
             for r, rank in ranks():
                 p_in = bank_tile(f"p_in{r}", PIECE)
-                nc.tensor.matmul(p_in[:], w2_sb[:, r * P : (r + 1) * P], h[c][:], start=True, stop=True)
+                nc.tensor.matmul(p_in[:], w2_in[:, r * P : (r + 1) * P], h[c][:], start=True, stop=True)
                 if r == R - 1 and 0 < c < N_PIECES - 1:
                     moved = work.tile([P, PIECE], F32, name="moved")
                     nc.scalar.activation(moved[:], p_in[:], IDENTITY, bias=b2_sb[:, r : r + 1])
@@ -94,13 +99,13 @@ def tile_stylehyperlinear_kernel(tc, styles, w1, b1, w2, b2, x, wb, bb, offs, ou
             p_out = bank_tile("p_out", R * PIECE)
             vec[c] = work.tile([P, R * PIECE], F32, name="vec")
             for r, rank in ranks():
-                nc.tensor.matmul(p_out[:, rank], w2_sb[:, (R + r) * P : (R + r + 1) * P], h[c][:], start=True, stop=True)
+                nc.tensor.matmul(p_out[:, rank], w2_out[:, r * P : (r + 1) * P], h[c][:], start=True, stop=True)
             for r, rank in ranks():
                 nc.scalar.activation(vec[c][:, rank], p_out[:, rank], IDENTITY, bias=b2_sb[:, R + r : R + r + 1])
 
         def sums_over_features(c):
             low[c] = bank_tile("low", R * PIECE)
-            nc.tensor.matmul(low[c][:], ones[:, 0:P], prod[c][:], start=True, stop=True)
+            nc.tensor.matmul(low[c][:], ones[:], prod[c][:], start=True, stop=True)
             base[c] = bank_tile("base", PIECE)
             nc.tensor.matmul(base[c][:], wb_sb[:], x_piece(c), start=True, stop=summer[c] != "tensor")
             if summer[c] == "gpsimd":

@@ -30,18 +30,14 @@ def tile_stylehyperlinear_kernel(tc, styles, w1, b1, w2, b2, x, wb, bb, offs, ou
         nc.sync.dma_start(w1_sb[:], w1)
         b1_sb = held.tile([P, 1], F32, name="b1_sb")
         nc.sync.dma_start(b1_sb[:], b1)
-        w2_in = held.tile([P, R * P], BF16, name="w2_in")
-        nc.sync.dma_start(w2_in[:], w2[:, 0 : R * P])
+        w2_sb = held.tile([P, 2 * R * P], BF16, name="w2_sb")
+        nc.sync.dma_start(w2_sb[:], w2)
         b2_sb = held.tile([P, 2 * R], F32, name="b2_sb")
         with nc.allow_non_contiguous_dma(reason="512 biases, one to a partition and block"):
             nc.sync.dma_start(b2_sb[:], b2.rearrange("(q p) one -> p (q one)", p=P))
-        x_cuts = [0, PIECE, 2 * PIECE, N]
-        x_sb = [held.tile([P, x_cuts[i + 1] - x_cuts[i]], BF16, name=f"x_sb{i}") for i in range(3)]
-        nc.sync.dma_start(x_sb[0][:], x[:, 0 : x_cuts[1]])
-        nc.gpsimd.dma_start(x_sb[1][:], x[:, x_cuts[1] : x_cuts[2]])
-        w2_out = held.tile([P, R * P], BF16, name="w2_out")
-        nc.sync.dma_start(w2_out[:], w2[:, R * P : 2 * R * P])
-        nc.gpsimd.dma_start(x_sb[2][:], x[:, x_cuts[2] : N])
+        x_half = [held.tile([P, N // 2], BF16, name=f"x_half{i}") for i in range(2)]
+        for i in range(2):
+            nc.sync.dma_start(x_half[i][:], x[:, i * (N // 2) : (i + 1) * (N // 2)])
         wb_sb = held.tile([P, P], BF16, name="wb_sb")
         nc.sync.dma_start(wb_sb[:], wb)
         bb_sb = held.tile([P, 1], F32, name="bb_sb")
@@ -73,9 +69,7 @@ def tile_stylehyperlinear_kernel(tc, styles, w1, b1, w2, b2, x, wb, bb, offs, ou
             return [(r, slice(r * PIECE, (r + 1) * PIECE)) for r in range(R)]
 
         def x_piece(c):
-            load = min(c, 2)
-            first = c * PIECE - x_cuts[load]
-            return x_sb[load][:, first : first + PIECE]
+            return x_half[c * PIECE // (N // 2)][:, c * PIECE % (N // 2) : c * PIECE % (N // 2) + PIECE]
 
         prod, vec, low, base, base_sb = {}, {}, {}, {}, {}
 
@@ -85,7 +79,7 @@ def tile_stylehyperlinear_kernel(tc, styles, w1, b1, w2, b2, x, wb, bb, offs, ou
             prod[c] = work.tile([P, R * PIECE], BF16, name="prod")
             for r, rank in ranks():
                 p_in = bank_tile(f"p_in{r}", PIECE)
-                nc.tensor.matmul(p_in[:], w2_in[:, r * P : (r + 1) * P], h[c][:], start=True, stop=True)
+                nc.tensor.matmul(p_in[:], w2_sb[:, r * P : (r + 1) * P], h[c][:], start=True, stop=True)
                 if r == R - 1 and 0 < c < N_PIECES - 1:
                     moved = work.tile([P, PIECE], F32, name="moved")
                     nc.scalar.activation(moved[:], p_in[:], IDENTITY, bias=b2_sb[:, r : r + 1])
@@ -99,7 +93,7 @@ def tile_stylehyperlinear_kernel(tc, styles, w1, b1, w2, b2, x, wb, bb, offs, ou
             p_out = bank_tile("p_out", R * PIECE)
             vec[c] = work.tile([P, R * PIECE], F32, name="vec")
             for r, rank in ranks():
-                nc.tensor.matmul(p_out[:, rank], w2_out[:, r * P : (r + 1) * P], h[c][:], start=True, stop=True)
+                nc.tensor.matmul(p_out[:, rank], w2_sb[:, (R + r) * P : (R + r + 1) * P], h[c][:], start=True, stop=True)
             for r, rank in ranks():
                 nc.scalar.activation(vec[c][:, rank], p_out[:, rank], IDENTITY, bias=b2_sb[:, R + r : R + r + 1])
 

@@ -5,8 +5,11 @@ P = 128
 S = 512
 N = 1024
 R = 2
-PIECE = 256
-N_PIECES = N // PIECE
+LOOK_UP = 256
+BANK = 512
+WIDTHS = [BANK // 2, BANK // 2, BANK]
+N_PIECES = len(WIDTHS)
+STARTS = [sum(WIDTHS[:c]) for c in range(N_PIECES)]
 WARM_UP = 12
 BF16, F32, U16 = mybir.dt.bfloat16, mybir.dt.float32, mybir.dt.uint16
 ADD, MULT = mybir.AluOpType.add, mybir.AluOpType.mult
@@ -19,7 +22,7 @@ def tile_stylehyperlinear_kernel(tc, styles, w1, b1, w2, b2, x, wb, bb, offs, ou
     nc = tc.nc
     with (
         tc.tile_pool(name="held", bufs=1) as held,
-        tc.tile_pool(name="work", bufs=N_PIECES) as work,
+        tc.tile_pool(name="work", bufs=1) as work,
         tc.psum_pool(name="psum", bufs=8) as psum,
     ):
         offsets = held.tile([P, N // 16], U16, name="offsets")
@@ -56,74 +59,101 @@ def tile_stylehyperlinear_kernel(tc, styles, w1, b1, w2, b2, x, wb, bb, offs, ou
         def bank_tile(name, columns):
             return psum.tile([P, columns], F32, name=name, tag="bank")
 
-        z = [bank_tile(f"z{c}", PIECE) for c in range(N_PIECES)]
-        for c in range(N_PIECES):
-            looked_up = bank[:].indirect(offsets[:, c * (PIECE // 16) : (c + 1) * (PIECE // 16)])
-            nc.tensor.matmul(z[c][:], w1_sb[:], looked_up, start=True, stop=True)
+        h = held.tile([P, N], BF16, name="h")
+        looks = [slice(first, first + LOOK_UP) for first in range(0, N, LOOK_UP)]
+        z = [bank_tile(f"z{i}", LOOK_UP) for i in range(len(looks))]
+        for i, look in enumerate(looks):
+            looked_up = bank[:].indirect(offsets[:, look.start // 16 : look.stop // 16])
+            nc.tensor.matmul(z[i][:], w1_sb[:], looked_up, start=True, stop=True)
+        for i, look in enumerate(looks):
+            nc.scalar.activation(h[:, look], z[i][:], SILU, bias=b1_sb[:])
 
-        h = [work.tile([P, PIECE], BF16, name="h") for c in range(N_PIECES)]
-        for c in range(N_PIECES):
-            nc.scalar.activation(h[c][:], z[c][:], SILU, bias=b1_sb[:])
+        def samples(c):
+            return slice(STARTS[c], STARTS[c] + WIDTHS[c])
 
-        def ranks():
-            return [(r, slice(r * PIECE, (r + 1) * PIECE)) for r in range(R)]
+        def of_rank(c, r):
+            return slice(r * WIDTHS[c], (r + 1) * WIDTHS[c])
+
+        def ranks_by_bank(c):
+            return [[0, 1]] if R * WIDTHS[c] <= BANK else [[0], [1]]
 
         def x_piece(c):
-            return x_half[c * PIECE // (N // 2)][:, c * PIECE % (N // 2) : c * PIECE % (N // 2) + PIECE]
+            half = STARTS[c] // (N // 2)
+            first = STARTS[c] - half * (N // 2)
+            return x_half[half][:, first : first + WIDTHS[c]]
 
         prod, vec, low, base, base_sb = {}, {}, {}, {}, {}
 
-        summer = ["vector" if c >= N_PIECES // 2 else "gpsimd" if c % 2 == 0 else "tensor" for c in range(N_PIECES)]
+        summer = ["gpsimd", "tensor", "vector"]
 
         def input_vectors(c):
-            prod[c] = work.tile([P, R * PIECE], BF16, name="prod")
-            for r, rank in ranks():
-                p_in = bank_tile(f"p_in{r}", PIECE)
-                nc.tensor.matmul(p_in[:], w2_sb[:, r * P : (r + 1) * P], h[c][:], start=True, stop=True)
+            prod[c] = work.tile([P, R * WIDTHS[c]], BF16, name=f"prod{c}")
+            for r in range(R):
+                p_in = bank_tile(f"p_in{r}", WIDTHS[c])
+                nc.tensor.matmul(p_in[:], w2_sb[:, r * P : (r + 1) * P], h[:, samples(c)], start=True, stop=True)
+                product = prod[c][:, of_rank(c, r)]
                 if r == R - 1 and 0 < c < N_PIECES - 1:
-                    moved = work.tile([P, PIECE], F32, name="moved")
+                    moved = work.tile([P, WIDTHS[c]], F32, name="moved")
                     nc.scalar.activation(moved[:], p_in[:], IDENTITY, bias=b2_sb[:, r : r + 1])
-                    nc.gpsimd.tensor_tensor(prod[c][:, rank], moved[:], x_piece(c), MULT)
+                    nc.gpsimd.tensor_tensor(product, moved[:], x_piece(c), MULT)
                 else:
                     nc.vector.scalar_tensor_tensor(
-                        prod[c][:, rank], p_in[:], b2_sb[:, r : r + 1], x_piece(c), op0=ADD, op1=MULT
+                        product, p_in[:], b2_sb[:, r : r + 1], x_piece(c), op0=ADD, op1=MULT
                     )
 
         def output_vectors(c):
-            p_out = bank_tile("p_out", R * PIECE)
-            vec[c] = work.tile([P, R * PIECE], F32, name="vec")
-            for r, rank in ranks():
-                nc.tensor.matmul(p_out[:, rank], w2_sb[:, (R + r) * P : (R + r + 1) * P], h[c][:], start=True, stop=True)
-            for r, rank in ranks():
-                nc.scalar.activation(vec[c][:, rank], p_out[:, rank], IDENTITY, bias=b2_sb[:, R + r : R + r + 1])
+            vec[c] = work.tile([P, R * WIDTHS[c]], F32, name=f"vec{c}")
+            for ranks in ranks_by_bank(c):
+                p_out = bank_tile("p_out", len(ranks) * WIDTHS[c])
+                for i, r in enumerate(ranks):
+                    w2_block = w2_sb[:, (R + r) * P : (R + r + 1) * P]
+                    nc.tensor.matmul(p_out[:, of_rank(c, i)], w2_block, h[:, samples(c)], start=True, stop=True)
+                for i, r in enumerate(ranks):
+                    bias = b2_sb[:, R + r : R + r + 1]
+                    nc.scalar.activation(vec[c][:, of_rank(c, r)], p_out[:, of_rank(c, i)], IDENTITY, bias=bias)
 
         def sums_over_features(c):
-            low[c] = bank_tile("low", R * PIECE)
-            nc.tensor.matmul(low[c][:], ones[:], prod[c][:], start=True, stop=True)
-            base[c] = bank_tile("base", PIECE)
+            low[c] = []
+            for ranks in ranks_by_bank(c):
+                columns = slice(ranks[0] * WIDTHS[c], (ranks[-1] + 1) * WIDTHS[c])
+                low_bank = bank_tile("low", len(ranks) * WIDTHS[c])
+                nc.tensor.matmul(low_bank[:], ones[:], prod[c][:, columns], start=True, stop=True)
+                low[c].append((low_bank, columns))
+            base[c] = bank_tile("base", WIDTHS[c])
             nc.tensor.matmul(base[c][:], wb_sb[:], x_piece(c), start=True, stop=summer[c] != "tensor")
             if summer[c] == "gpsimd":
-                base_sb[c] = work.tile([P, PIECE], F32, name="base_sb")
+                base_sb[c] = work.tile([P, WIDTHS[c]], F32, name="base_sb")
                 nc.scalar.activation(base_sb[c][:], base[c][:], IDENTITY, bias=bb_sb[:])
 
         def finish(c):
-            term = work.tile([P, R * PIECE], F32, name="term")
-            nc.vector.tensor_tensor(term[:], low[c][:], vec[c][:], MULT)
-            res = work.tile([P, PIECE], F32, name="res")
+            term = work.tile([P, R * WIDTHS[c]], F32, name=f"term{c}")
+            for low_bank, columns in low[c]:
+                nc.vector.tensor_tensor(term[:, columns], low_bank[:], vec[c][:, columns], MULT)
+            term_0, term_1 = term[:, of_rank(c, 0)], term[:, of_rank(c, 1)]
+            res = work.tile([P, WIDTHS[c]], F32, name=f"res{c}")
             if summer[c] == "tensor":
-                for r, rank in ranks():
-                    nc.tensor.matmul(base[c][:], identity[:], term[:, rank], start=False, stop=r == R - 1)
+                nc.tensor.matmul(base[c][:], identity[:], term_0, start=False, stop=False)
+                nc.tensor.matmul(base[c][:], identity[:], term_1, start=False, stop=True)
                 nc.scalar.activation(res[:], base[c][:], IDENTITY, bias=bb_sb[:])
+                nc.sync.dma_start(out[:, samples(c)], res[:])
             elif summer[c] == "gpsimd":
-                delta = work.tile([P, PIECE], F32, name="delta")
-                nc.gpsimd.tensor_tensor(delta[:], term[:, 0:PIECE], term[:, PIECE : 2 * PIECE], ADD)
+                delta = work.tile([P, WIDTHS[c]], F32, name="delta")
+                nc.gpsimd.tensor_tensor(delta[:], term_0, term_1, ADD)
                 nc.gpsimd.tensor_tensor(res[:], delta[:], base_sb[c][:], ADD)
+                nc.sync.dma_start(out[:, samples(c)], res[:])
             else:
-                part = work.tile([P, PIECE], F32, name="part")
-                nc.vector.scalar_tensor_tensor(part[:], base[c][:], bb_sb[:], term[:, 0:PIECE], op0=ADD, op1=ADD)
-                adder = nc.gpsimd if c + 1 < N_PIECES else nc.vector
-                adder.tensor_tensor(res[:], part[:], term[:, PIECE : 2 * PIECE], ADD)
-            nc.sync.dma_start(out[:, c * PIECE : (c + 1) * PIECE], res[:])
+                part = work.tile([P, WIDTHS[c]], F32, name="part")
+                half = WIDTHS[c] // 2
+                for first in (0, half):
+                    cut = slice(first, first + half)
+                    nc.vector.scalar_tensor_tensor(
+                        part[:, cut], base[c][:, cut], bb_sb[:], term[:, first : first + half], op0=ADD, op1=ADD
+                    )
+                for first in (0, half):
+                    cut = slice(first, first + half)
+                    second_rank = slice(WIDTHS[c] + first, WIDTHS[c] + first + half)
+                    nc.vector.tensor_tensor(res[:, cut], part[:, cut], term[:, second_rank], ADD)
+                    nc.sync.dma_start(out[:, STARTS[c] + first : STARTS[c] + first + half], res[:, cut])
 
         stages = [input_vectors, output_vectors, sums_over_features, finish]
         for step in range(N_PIECES + len(stages) - 1):

@@ -1,5 +1,4 @@
 import concourse.mybir as mybir
-from concourse.masks import make_identity
 
 P = 128
 S = 512
@@ -7,7 +6,8 @@ N = 1024
 R = 2
 LOOK_UP = 256
 BANK = 512
-WIDTHS = [BANK // 2, BANK // 2, BANK]
+WIDE = BANK // 2
+WIDTHS = [WIDE, WIDE, WIDE, WIDE // 2, WIDE // 2]
 N_PIECES = len(WIDTHS)
 STARTS = [sum(WIDTHS[:c]) for c in range(N_PIECES)]
 WARM_UP = 12
@@ -50,8 +50,6 @@ def tile_stylehyperlinear_kernel(tc, styles, w1, b1, w2, b2, x, wb, bb, offs, ou
         nc.vector.memset(ones[:], 1.0)
         scratch = held.tile([P, 1], BF16, name="scratch")
         nc.scalar.activation(scratch[:], ones[:, 0:1], SILU)
-        identity = held.tile([P, P], F32, name="identity")
-        make_identity(nc, identity[:])
         idle = psum.tile([P, P], F32, name="idle", tag="bank")
         for i in range(WARM_UP):
             nc.tensor.matmul(idle[:], ones[:], ones[:], start=True, stop=True)
@@ -74,89 +72,64 @@ def tile_stylehyperlinear_kernel(tc, styles, w1, b1, w2, b2, x, wb, bb, offs, ou
         def of_rank(c, r):
             return slice(r * WIDTHS[c], (r + 1) * WIDTHS[c])
 
-        def ranks_by_bank(c):
-            return [[0, 1]] if R * WIDTHS[c] <= BANK else [[0], [1]]
-
         def x_piece(c):
             half = STARTS[c] // (N // 2)
             first = STARTS[c] - half * (N // 2)
             return x_half[half][:, first : first + WIDTHS[c]]
 
-        prod, vec, low, base, base_sb = {}, {}, {}, {}, {}
-
-        summer = ["gpsimd", "tensor", "vector"]
+        prod, vec, low, base, term, delta = {}, {}, {}, {}, {}, {}
 
         def input_vectors(c):
             prod[c] = work.tile([P, R * WIDTHS[c]], BF16, name=f"prod{c}")
             for r in range(R):
                 p_in = bank_tile(f"p_in{r}", WIDTHS[c])
                 nc.tensor.matmul(p_in[:], w2_sb[:, r * P : (r + 1) * P], h[:, samples(c)], start=True, stop=True)
-                product = prod[c][:, of_rank(c, r)]
-                if r == R - 1 and 0 < c < N_PIECES - 1:
-                    moved = work.tile([P, WIDTHS[c]], F32, name="moved")
-                    nc.scalar.activation(moved[:], p_in[:], IDENTITY, bias=b2_sb[:, r : r + 1])
-                    nc.gpsimd.tensor_tensor(product, moved[:], x_piece(c), MULT)
-                else:
-                    nc.vector.scalar_tensor_tensor(
-                        product, p_in[:], b2_sb[:, r : r + 1], x_piece(c), op0=ADD, op1=MULT
-                    )
+                nc.vector.scalar_tensor_tensor(
+                    prod[c][:, of_rank(c, r)], p_in[:], b2_sb[:, r : r + 1], x_piece(c), op0=ADD, op1=MULT
+                )
 
         def output_vectors(c):
             vec[c] = work.tile([P, R * WIDTHS[c]], F32, name=f"vec{c}")
-            for ranks in ranks_by_bank(c):
-                p_out = bank_tile("p_out", len(ranks) * WIDTHS[c])
-                for i, r in enumerate(ranks):
-                    w2_block = w2_sb[:, (R + r) * P : (R + r + 1) * P]
-                    nc.tensor.matmul(p_out[:, of_rank(c, i)], w2_block, h[:, samples(c)], start=True, stop=True)
-                for i, r in enumerate(ranks):
-                    bias = b2_sb[:, R + r : R + r + 1]
-                    nc.scalar.activation(vec[c][:, of_rank(c, r)], p_out[:, of_rank(c, i)], IDENTITY, bias=bias)
+            p_out = bank_tile("p_out", R * WIDTHS[c])
+            for r in range(R):
+                w2_block = w2_sb[:, (R + r) * P : (R + r + 1) * P]
+                nc.tensor.matmul(p_out[:, of_rank(c, r)], w2_block, h[:, samples(c)], start=True, stop=True)
+            for r in range(R):
+                bias = b2_sb[:, R + r : R + r + 1]
+                nc.scalar.activation(vec[c][:, of_rank(c, r)], p_out[:, of_rank(c, r)], IDENTITY, bias=bias)
 
         def sums_over_features(c):
-            low[c] = []
-            for ranks in ranks_by_bank(c):
-                columns = slice(ranks[0] * WIDTHS[c], (ranks[-1] + 1) * WIDTHS[c])
-                low_bank = bank_tile("low", len(ranks) * WIDTHS[c])
-                nc.tensor.matmul(low_bank[:], ones[:], prod[c][:, columns], start=True, stop=True)
-                low[c].append((low_bank, columns))
+            low[c] = bank_tile("low", R * WIDTHS[c])
+            nc.tensor.matmul(low[c][:], ones[:], prod[c][:], start=True, stop=True)
+
+        def shared_layer(c):
             base[c] = bank_tile("base", WIDTHS[c])
-            nc.tensor.matmul(base[c][:], wb_sb[:], x_piece(c), start=True, stop=summer[c] != "tensor")
-            if summer[c] == "gpsimd":
-                base_sb[c] = work.tile([P, WIDTHS[c]], F32, name="base_sb")
-                nc.scalar.activation(base_sb[c][:], base[c][:], IDENTITY, bias=bb_sb[:])
+            nc.tensor.matmul(base[c][:], wb_sb[:], x_piece(c), start=True, stop=True)
+
+        def multiply(c):
+            term[c] = work.tile([P, R * WIDTHS[c]], F32, name=f"term{c}")
+            nc.vector.tensor_tensor(term[c][:], low[c][:], vec[c][:], MULT)
+
+        def add_terms(c):
+            delta[c] = work.tile([P, WIDTHS[c]], F32, name=f"delta{c}")
+            adder = nc.gpsimd if WIDTHS[c] == WIDE else nc.vector
+            adder.tensor_tensor(delta[c][:], term[c][:, of_rank(c, 0)], term[c][:, of_rank(c, 1)], ADD)
 
         def finish(c):
-            term = work.tile([P, R * WIDTHS[c]], F32, name=f"term{c}")
-            for low_bank, columns in low[c]:
-                nc.vector.tensor_tensor(term[:, columns], low_bank[:], vec[c][:, columns], MULT)
-            term_0, term_1 = term[:, of_rank(c, 0)], term[:, of_rank(c, 1)]
             res = work.tile([P, WIDTHS[c]], F32, name=f"res{c}")
-            if summer[c] == "tensor":
-                nc.tensor.matmul(base[c][:], identity[:], term_0, start=False, stop=False)
-                nc.tensor.matmul(base[c][:], identity[:], term_1, start=False, stop=True)
-                nc.scalar.activation(res[:], base[c][:], IDENTITY, bias=bb_sb[:])
-                nc.sync.dma_start(out[:, samples(c)], res[:])
-            elif summer[c] == "gpsimd":
-                delta = work.tile([P, WIDTHS[c]], F32, name="delta")
-                nc.gpsimd.tensor_tensor(delta[:], term_0, term_1, ADD)
-                nc.gpsimd.tensor_tensor(res[:], delta[:], base_sb[c][:], ADD)
-                nc.sync.dma_start(out[:, samples(c)], res[:])
-            else:
-                part = work.tile([P, WIDTHS[c]], F32, name="part")
-                half = WIDTHS[c] // 2
-                for first in (0, half):
-                    cut = slice(first, first + half)
-                    nc.vector.scalar_tensor_tensor(
-                        part[:, cut], base[c][:, cut], bb_sb[:], term[:, first : first + half], op0=ADD, op1=ADD
-                    )
-                for first in (0, half):
-                    cut = slice(first, first + half)
-                    second_rank = slice(WIDTHS[c] + first, WIDTHS[c] + first + half)
-                    nc.vector.tensor_tensor(res[:, cut], part[:, cut], term[:, second_rank], ADD)
-                    nc.sync.dma_start(out[:, STARTS[c] + first : STARTS[c] + first + half], res[:, cut])
+            nc.vector.scalar_tensor_tensor(res[:], base[c][:], bb_sb[:], delta[c][:], op0=ADD, op1=ADD)
+            nc.sync.dma_start(out[:, samples(c)], res[:])
 
-        stages = [input_vectors, output_vectors, sums_over_features, finish]
-        for step in range(N_PIECES + len(stages) - 1):
-            for behind, stage in enumerate(stages):
+        stages = [
+            (input_vectors, 0),
+            (sums_over_features, 2),
+            (output_vectors, 1),
+            (shared_layer, 3),
+            (multiply, 2),
+            (add_terms, 3),
+            (finish, 4),
+        ]
+        for step in range(N_PIECES + stages[-1][1]):
+            for stage, behind in stages:
                 if 0 <= step - behind < N_PIECES:
                     stage(step - behind)

@@ -1,15 +1,17 @@
 import concourse.mybir as mybir
+from concourse.masks import make_identity
 
 P = 128
 S = 512
 N = 1024
 R = 2
-LOOK_UP = 256
 BANK = 512
 WIDE = BANK // 2
 WIDTHS = [WIDE, WIDE, WIDE, WIDE // 2, WIDE // 2]
+LOOK_UP = WIDE
 N_PIECES = len(WIDTHS)
 STARTS = [sum(WIDTHS[:c]) for c in range(N_PIECES)]
+X_CUT = STARTS[2]
 WARM_UP = 12
 BF16, F32, U16 = mybir.dt.bfloat16, mybir.dt.float32, mybir.dt.uint16
 ADD, MULT = mybir.AluOpType.add, mybir.AluOpType.mult
@@ -38,9 +40,10 @@ def tile_stylehyperlinear_kernel(tc, styles, w1, b1, w2, b2, x, wb, bb, offs, ou
         b2_sb = held.tile([P, 2 * R], F32, name="b2_sb")
         with nc.allow_non_contiguous_dma(reason="512 biases, one to a partition and block"):
             nc.sync.dma_start(b2_sb[:], b2.rearrange("(q p) one -> p (q one)", p=P))
-        x_half = [held.tile([P, N // 2], BF16, name=f"x_half{i}") for i in range(2)]
-        for i in range(2):
-            nc.sync.dma_start(x_half[i][:], x[:, i * (N // 2) : (i + 1) * (N // 2)])
+        x_early = held.tile([P, X_CUT], BF16, name="x_early")
+        nc.sync.dma_start(x_early[:], x[:, 0:X_CUT])
+        x_late = held.tile([P, N - X_CUT], BF16, name="x_late")
+        nc.sync.dma_start(x_late[:], x[:, X_CUT:N])
         wb_sb = held.tile([P, P], BF16, name="wb_sb")
         nc.sync.dma_start(wb_sb[:], wb)
         bb_sb = held.tile([P, 1], F32, name="bb_sb")
@@ -50,12 +53,17 @@ def tile_stylehyperlinear_kernel(tc, styles, w1, b1, w2, b2, x, wb, bb, offs, ou
         nc.vector.memset(ones[:], 1.0)
         scratch = held.tile([P, 1], BF16, name="scratch")
         nc.scalar.activation(scratch[:], ones[:, 0:1], SILU)
+        identity = held.tile([P, P], F32, name="identity")
+        make_identity(nc, identity[:])
         idle = psum.tile([P, P], F32, name="idle", tag="bank")
         for i in range(WARM_UP):
             nc.tensor.matmul(idle[:], ones[:], ones[:], start=True, stop=True)
 
         def bank_tile(name, columns):
             return psum.tile([P, columns], F32, name=name, tag="bank")
+
+        def samples(c):
+            return slice(STARTS[c], STARTS[c] + WIDTHS[c])
 
         h = held.tile([P, N], BF16, name="h")
         looks = [slice(first, first + LOOK_UP) for first in range(0, N, LOOK_UP)]
@@ -66,18 +74,16 @@ def tile_stylehyperlinear_kernel(tc, styles, w1, b1, w2, b2, x, wb, bb, offs, ou
         for i, look in enumerate(looks):
             nc.scalar.activation(h[:, look], z[i][:], SILU, bias=b1_sb[:])
 
-        def samples(c):
-            return slice(STARTS[c], STARTS[c] + WIDTHS[c])
-
         def of_rank(c, r):
             return slice(r * WIDTHS[c], (r + 1) * WIDTHS[c])
 
         def x_piece(c):
-            half = STARTS[c] // (N // 2)
-            first = STARTS[c] - half * (N // 2)
-            return x_half[half][:, first : first + WIDTHS[c]]
+            part, first = (x_early, STARTS[c]) if STARTS[c] < X_CUT else (x_late, STARTS[c] - X_CUT)
+            return part[:, first : first + WIDTHS[c]]
 
-        prod, vec, low, base, term, delta = {}, {}, {}, {}, {}, {}
+        adder = ["gpsimd"] * (N_PIECES - 2) + ["tensor", "vector"]
+
+        prod, vec, low, base, term, rest = {}, {}, {}, {}, {}, {}
 
         def input_vectors(c):
             prod[c] = work.tile([P, R * WIDTHS[c]], BF16, name=f"prod{c}")
@@ -104,20 +110,26 @@ def tile_stylehyperlinear_kernel(tc, styles, w1, b1, w2, b2, x, wb, bb, offs, ou
 
         def shared_layer(c):
             base[c] = bank_tile("base", WIDTHS[c])
-            nc.tensor.matmul(base[c][:], wb_sb[:], x_piece(c), start=True, stop=True)
+            nc.tensor.matmul(base[c][:], wb_sb[:], x_piece(c), start=True, stop=adder[c] != "tensor")
 
         def multiply(c):
             term[c] = work.tile([P, R * WIDTHS[c]], F32, name=f"term{c}")
             nc.vector.tensor_tensor(term[c][:], low[c][:], vec[c][:], MULT)
 
-        def add_terms(c):
-            delta[c] = work.tile([P, WIDTHS[c]], F32, name=f"delta{c}")
-            adder = nc.gpsimd if WIDTHS[c] == WIDE else nc.vector
-            adder.tensor_tensor(delta[c][:], term[c][:, of_rank(c, 0)], term[c][:, of_rank(c, 1)], ADD)
+        def first_add(c):
+            term_0, term_1 = term[c][:, of_rank(c, 0)], term[c][:, of_rank(c, 1)]
+            if adder[c] == "tensor":
+                nc.tensor.matmul(base[c][:], identity[:], term_0, start=False, stop=True)
+                rest[c] = term_1
+            else:
+                engine = nc.gpsimd if adder[c] == "gpsimd" else nc.vector
+                delta = work.tile([P, WIDTHS[c]], F32, name=f"delta{c}")
+                engine.tensor_tensor(delta[:], term_0, term_1, ADD)
+                rest[c] = delta[:]
 
-        def finish(c):
+        def last_add(c):
             res = work.tile([P, WIDTHS[c]], F32, name=f"res{c}")
-            nc.vector.scalar_tensor_tensor(res[:], base[c][:], bb_sb[:], delta[c][:], op0=ADD, op1=ADD)
+            nc.vector.scalar_tensor_tensor(res[:], base[c][:], bb_sb[:], rest[c], op0=ADD, op1=ADD)
             nc.sync.dma_start(out[:, samples(c)], res[:])
 
         stages = [
@@ -126,8 +138,8 @@ def tile_stylehyperlinear_kernel(tc, styles, w1, b1, w2, b2, x, wb, bb, offs, ou
             (output_vectors, 1),
             (shared_layer, 3),
             (multiply, 2),
-            (add_terms, 3),
-            (finish, 4),
+            (first_add, 3),
+            (last_add, 4),
         ]
         for step in range(N_PIECES + stages[-1][1]):
             for stage, behind in stages:

@@ -11,7 +11,7 @@ WIDTHS = [WIDE, WIDE, WIDE, WIDE // 2, WIDE // 2]
 LOOK_UP = WIDE
 N_PIECES = len(WIDTHS)
 STARTS = [sum(WIDTHS[:c]) for c in range(N_PIECES)]
-X_CUT = STARTS[2]
+X_CUT = STARTS[1]
 WARM_UP = 12
 BF16, F32, U16 = mybir.dt.bfloat16, mybir.dt.float32, mybir.dt.uint16
 ADD, MULT = mybir.AluOpType.add, mybir.AluOpType.mult
@@ -27,10 +27,10 @@ def tile_stylehyperlinear_kernel(tc, styles, w1, b1, w2, b2, x, wb, bb, offs, ou
         tc.tile_pool(name="work", bufs=1) as work,
         tc.psum_pool(name="psum", bufs=8) as psum,
     ):
-        offsets = held.tile([P, N // 16], U16, name="offsets")
-        nc.sync.dma_start(offsets[:], offs)
         bank = held.tile([P, S], BF16, name="bank")
         nc.sync.dma_start(bank[:], styles)
+        offsets = held.tile([P, N // 16], U16, name="offsets")
+        nc.sync.dma_start(offsets[:], offs)
         w1_sb = held.tile([P, P], BF16, name="w1_sb")
         nc.sync.dma_start(w1_sb[:], w1)
         b1_sb = held.tile([P, 1], F32, name="b1_sb")

import concourse.mybir as mybir
from concourse.masks import make_identity

P = 128
S = 512
N = 1024
R = 2
BANK = 512
WIDE = BANK // 2
WIDTHS = [WIDE, WIDE, WIDE, WIDE // 2, WIDE // 2]
LOOK_UP = WIDE
N_PIECES = len(WIDTHS)
STARTS = [sum(WIDTHS[:c]) for c in range(N_PIECES)]
X_CUT = STARTS[1]
WARM_UP = 12
BF16, F32, U16 = mybir.dt.bfloat16, mybir.dt.float32, mybir.dt.uint16
ADD, MULT = mybir.AluOpType.add, mybir.AluOpType.mult
SILU, IDENTITY = mybir.ActivationFunctionType.Silu, mybir.ActivationFunctionType.Identity

FLOPS = 2 * N * (P * P + P * 2 * R * P + P * P) + 4 * R * P * N


def tile_stylehyperlinear_kernel(tc, styles, w1, b1, w2, b2, x, wb, bb, offs, out):
    nc = tc.nc
    with (
        tc.tile_pool(name="held", bufs=1) as held,
        tc.tile_pool(name="work", bufs=1) as work,
        tc.psum_pool(name="psum", bufs=8) as psum,
    ):
        bank = held.tile([P, S], BF16, name="bank")
        nc.sync.dma_start(bank[:], styles)
        offsets = held.tile([P, N // 16], U16, name="offsets")
        nc.sync.dma_start(offsets[:], offs)
        w1_sb = held.tile([P, P], BF16, name="w1_sb")
        nc.sync.dma_start(w1_sb[:], w1)
        b1_sb = held.tile([P, 1], F32, name="b1_sb")
        nc.sync.dma_start(b1_sb[:], b1)
        w2_sb = held.tile([P, 2 * R * P], BF16, name="w2_sb")
        nc.sync.dma_start(w2_sb[:], w2)
        b2_sb = held.tile([P, 2 * R], F32, name="b2_sb")
        with nc.allow_non_contiguous_dma(reason="512 biases, one to a partition and block"):
            nc.sync.dma_start(b2_sb[:], b2.rearrange("(q p) one -> p (q one)", p=P))
        x_early = held.tile([P, X_CUT], BF16, name="x_early")
        nc.sync.dma_start(x_early[:], x[:, 0:X_CUT])
        x_late = held.tile([P, N - X_CUT], BF16, name="x_late")
        nc.sync.dma_start(x_late[:], x[:, X_CUT:N])
        wb_sb = held.tile([P, P], BF16, name="wb_sb")
        nc.sync.dma_start(wb_sb[:], wb)
        bb_sb = held.tile([P, 1], F32, name="bb_sb")
        nc.sync.dma_start(bb_sb[:], bb)

        ones = held.tile([P, P], BF16, name="ones")
        nc.vector.memset(ones[:], 1.0)
        scratch = held.tile([P, 1], BF16, name="scratch")
        nc.scalar.activation(scratch[:], ones[:, 0:1], SILU)
        identity = held.tile([P, P], F32, name="identity")
        make_identity(nc, identity[:])
        idle = psum.tile([P, P], F32, name="idle", tag="bank")
        for i in range(WARM_UP):
            nc.tensor.matmul(idle[:], ones[:], ones[:], start=True, stop=True)

        def bank_tile(name, columns):
            return psum.tile([P, columns], F32, name=name, tag="bank")

        def samples(c):
            return slice(STARTS[c], STARTS[c] + WIDTHS[c])

        h = held.tile([P, N], BF16, name="h")
        looks = [slice(first, first + LOOK_UP) for first in range(0, N, LOOK_UP)]
        z = [bank_tile(f"z{i}", LOOK_UP) for i in range(len(looks))]
        for i, look in enumerate(looks):
            looked_up = bank[:].indirect(offsets[:, look.start // 16 : look.stop // 16])
            nc.tensor.matmul(z[i][:], w1_sb[:], looked_up, start=True, stop=True)
        for i, look in enumerate(looks):
            nc.scalar.activation(h[:, look], z[i][:], SILU, bias=b1_sb[:])

        def of_rank(c, r):
            return slice(r * WIDTHS[c], (r + 1) * WIDTHS[c])

        def x_piece(c):
            part, first = (x_early, STARTS[c]) if STARTS[c] < X_CUT else (x_late, STARTS[c] - X_CUT)
            return part[:, first : first + WIDTHS[c]]

        adder = ["gpsimd"] * (N_PIECES - 2) + ["tensor", "vector"]

        prod, vec, low, base, term, rest = {}, {}, {}, {}, {}, {}

        def input_vectors(c):
            prod[c] = work.tile([P, R * WIDTHS[c]], BF16, name=f"prod{c}")
            for r in range(R):
                p_in = bank_tile(f"p_in{r}", WIDTHS[c])
                nc.tensor.matmul(p_in[:], w2_sb[:, r * P : (r + 1) * P], h[:, samples(c)], start=True, stop=True)
                nc.vector.scalar_tensor_tensor(
                    prod[c][:, of_rank(c, r)], p_in[:], b2_sb[:, r : r + 1], x_piece(c), op0=ADD, op1=MULT
                )

        def output_vectors(c):
            vec[c] = work.tile([P, R * WIDTHS[c]], F32, name=f"vec{c}")
            p_out = bank_tile("p_out", R * WIDTHS[c])
            for r in range(R):
                w2_block = w2_sb[:, (R + r) * P : (R + r + 1) * P]
                nc.tensor.matmul(p_out[:, of_rank(c, r)], w2_block, h[:, samples(c)], start=True, stop=True)
            for r in range(R):
                bias = b2_sb[:, R + r : R + r + 1]
                nc.scalar.activation(vec[c][:, of_rank(c, r)], p_out[:, of_rank(c, r)], IDENTITY, bias=bias)

        def sums_over_features(c):
            low[c] = bank_tile("low", R * WIDTHS[c])
            nc.tensor.matmul(low[c][:], ones[:], prod[c][:], start=True, stop=True)

        def shared_layer(c):
            base[c] = bank_tile("base", WIDTHS[c])
            nc.tensor.matmul(base[c][:], wb_sb[:], x_piece(c), start=True, stop=adder[c] != "tensor")

        def multiply(c):
            term[c] = work.tile([P, R * WIDTHS[c]], F32, name=f"term{c}")
            nc.vector.tensor_tensor(term[c][:], low[c][:], vec[c][:], MULT)

        def first_add(c):
            term_0, term_1 = term[c][:, of_rank(c, 0)], term[c][:, of_rank(c, 1)]
            if adder[c] == "tensor":
                nc.tensor.matmul(base[c][:], identity[:], term_0, start=False, stop=True)
                rest[c] = term_1
            else:
                engine = nc.gpsimd if adder[c] == "gpsimd" else nc.vector
                delta = work.tile([P, WIDTHS[c]], F32, name=f"delta{c}")
                engine.tensor_tensor(delta[:], term_0, term_1, ADD)
                rest[c] = delta[:]

        def last_add(c):
            res = work.tile([P, WIDTHS[c]], F32, name=f"res{c}")
            nc.vector.scalar_tensor_tensor(res[:], base[c][:], bb_sb[:], rest[c], op0=ADD, op1=ADD)
            nc.sync.dma_start(out[:, samples(c)], res[:])

        stages = [
            (input_vectors, 0),
            (sums_over_features, 2),
            (output_vectors, 1),
            (shared_layer, 3),
            (multiply, 2),
            (first_add, 3),
            (last_add, 4),
        ]
        for step in range(N_PIECES + stages[-1][1]):
            for stage, behind in stages:
                if 0 <= step - behind < N_PIECES:
                    stage(step - behind)
